import numpy as np
import ml_dtypes


def mxq(x, axis, fmt="e4m3"):
    dtype, down = {"e4m3": (ml_dtypes.float8_e4m3fn, 7), "e5m2": (ml_dtypes.float8_e5m2, 14)}[fmt]
    v = np.moveaxis(np.asarray(x, np.float32).astype(ml_dtypes.bfloat16).astype(np.float64), axis, -1)
    blocks = v.reshape(v.shape[:-1] + (-1, 32))
    amax = np.abs(blocks).max(-1, keepdims=True)
    byte = np.maximum(np.where(amax > 0, np.frexp(amax)[1] - 1 + 127, 0) - down, 1)
    scale = np.exp2(byte - 127.0)
    codes = (blocks / scale).astype(np.float32).astype(dtype).astype(np.float64)
    return np.moveaxis((codes * scale).reshape(v.shape), -1, axis)


WIDE = False


def mx_kscale(k):
    if not WIDE:
        return np.ones(k)
    levels = np.array([10, -10, 5, -5, 0])
    if k % 512:
        return np.exp2(np.random.permutation(np.resize(levels, k // 32))).repeat(32)
    a = np.empty((k // 512, 16))
    for p in range(k // 512):
        a[p, :8] = np.random.permutation(np.resize(levels, 8))
        for g in range(8):
            far = levels[np.abs(levels - a[p, g]) >= 10]
            a[p, g + 8] = far[np.random.randint(len(far))]
    return np.exp2(a.ravel()).repeat(32)


BF16 = ml_dtypes.bfloat16


def bf(x):
    return np.asarray(x, np.float32).astype(BF16)


def f64(x):
    return np.asarray(x).astype(np.float64)


N, D, HOP = 1024, 512, 2
NW = HOP + 1


def setup_inputs():
    s = mx_kscale(N)
    u = s / s.min()
    g = u[None, :] / u[:, None]
    return {"A_p": bf(np.random.standard_normal((N, N)) / np.sqrt(N) * g),
            "x_p": bf(np.random.standard_normal((N, D)) / u[:, None]),
            "w_p": bf(1.0 + 0.1 * np.random.standard_normal((NW, 1)))}


def reference(A_p, x_p, w_p):
    ap = mxq(f64(A_p), 1, "e4m3")
    x = f64(x_p)
    wa, wb, wc = f64(w_p)
    feat_p = wa * x
    h1 = ap @ mxq(x, 0, "e4m3")
    feat_p = feat_p + wb * h1
    feat_p = feat_p + wc * (ap @ mxq(h1, 0, "e4m3"))
    return feat_p

@@ -1,0 +1,289 @@
+from contextlib import ExitStack
+
+import concourse.mybir as mybir
+from concourse.masks import make_identity
+
+F32 = mybir.dt.float32
+BF16 = mybir.dt.bfloat16
+U32 = mybir.dt.uint32
+U8 = mybir.dt.uint8
+FP8X4 = mybir.dt.float8_e4m3fn_x4
+ALU = mybir.AluOpType
+ACT = mybir.ActivationFunctionType
+
+P = 128
+N = 1024
+D = 512
+FLOPS = 2 * 2 * N * N * D
+
+PIN = True
+XS = 256
+GSPLIT = 1
+ATC_ENG = "SSSSSSSS"
+H1C_ENG = {(1, 0): "S", (1, 1): "V", (1, 2): "S", (1, 3): "V", (0, 0): "S", (0, 1): "S", (0, 2): "S", (0, 3): "S"}
+W0X_ENG = {(1, 0): "V", (1, 1): "V", (0, 0): "V", (0, 1): "V"}
+ACC_PATH = {(1, 0): "G", (1, 1): "G", (1, 2): "G", (1, 3): "G", (0, 0): "V", (0, 1): "V", (0, 2): "V", (0, 3): "G"}
+FIN_PATH = {(1, 0): "V", (1, 1): "V", (1, 2): "V", (1, 3): "V", (0, 0): "V", (0, 1): "V", (0, 2): "V", (0, 3): "V"}
+T_BANK = [4, 5, 6, 7, 4, 5, 6, 7]
+H_BANK = {(1, 0): 4, (1, 1): 5, (1, 2): 6, (1, 3): 7, (0, 0): 0, (0, 1): 1, (0, 2): 2, (0, 3): 3}
+O_BANK = {(1, 0): 2, (1, 1): 3, (1, 2): 6, (1, 3): 7, (0, 0): 0, (0, 1): 1, (0, 2): 4, (0, 3): 5}
+W_BANK = 3
+LOADS = ["x0", "x1", "A0", "A1", "A2", "A3"]
+ORDER = [
+    "w0x01", "xrgV0", "W0", "W0", "W0", "W1", "W1", "T0", "T1", "W1", "xrgS0", "xrgS1",
+    "T2", "ATc0", "xq0", "ATc1", "w0x11", "w0x10", "xrgV1", "xq1", "T3", "W1", "ATc2", "T4",
+    "Aq0", "T5", "W1", "M0b2", "ATc3", "ATc4", "Aq1", "M1b3", "ATc5", "T7", "T6", "M2b2",
+    "M2b3", "M0b3", "M3b3", "ATc7", "w0x00", "Aq2", "ATc6", "M1b2", "Aq3", "M3b2", "h1w03", "acc02",
+    "h1c03", "M1b1", "M4b2", "M2b0", "M5b3", "h1c02", "M5b2", "M4b3", "M6b3", "M7b3", "M0b0", "M7b2",
+    "M6b2", "M1b0", "h1c13", "h1c12", "M3b0", "h1w12", "M5b1", "M3b1", "hq01", "M2b1", "M0b1", "M6b1",
+    "h1c01", "acc03", "acc00", "M7b1", "M4b1", "M7b0", "M6b0", "M5b0", "h1w13", "M4b0", "h1c10", "hq11",
+    "h1c11", "O10", "acc12", "h1c00", "h1w11", "acc01", "acc13", "O11", "O12", "O13", "fin10", "st10",
+    "fin11", "st11", "hq10", "acc11", "hq00", "h1w10", "O00", "fin12", "st12", "acc10", "fin13", "st13",
+    "O01", "fin00", "st00", "O03", "fin01", "st01", "O02", "fin03", "st03", "fin02", "st02",
+]
+
+
+def tile_simpa_pb_kernel(tc, A_p, x_p, w_p, out):
+    nc = tc.nc
+    with ExitStack() as ctx:
+        keep = ctx.enter_context(tc.tile_pool(name="keep", bufs=1))
+        psum = ctx.enter_context(tc.psum_pool(name="psum", bufs=1))
+        if PIN:
+            ctx.enter_context(tc.manual_schedule())
+
+        def copy_on(eng, dst, src):
+            if eng == "S":
+                nc.scalar.copy(out=dst, in_=src)
+            else:
+                nc.vector.tensor_copy(out=dst, in_=src)
+
+        w_bf = keep.tile([P, 3], BF16, name="w_bf")
+        nc.scalar.dma_start(out=w_bf[:], in_=w_p.rearrange("a b -> (a b)").partition_broadcast(P))
+        x_sb = {}
+        a_sb = {}
+        for name in LOADS:
+            i = int(name[1])
+            if name[0] == "x":
+                xt = keep.tile([P, 4, D], BF16, name="x_sb%d" % i)
+                nc.sync.dma_start(
+                    out=xt[:].rearrange("p t d -> p (t d)"),
+                    in_=x_p[512 * i : 512 * (i + 1), :].rearrange("(p t) d -> p (t d)", t=4),
+                )
+                x_sb[i] = xt
+            else:
+                at = keep.tile([P, 2, N], BF16, name="a_sb%d" % i)
+                g, u = divmod(i, 2)
+                nc.sync.dma_start(
+                    out=at[:].rearrange("p e j -> p (e j)"),
+                    in_=A_p[512 * g : 512 * (g + 1), :].rearrange("(p u e) j -> p u (e j)", u=2, e=2)[:, u, :],
+                )
+                a_sb[i] = at
+        ident = keep.tile([P, P], F32, name="ident")
+        make_identity(nc, ident[:])
+        w_f = keep.tile([P, 3], F32, name="w_f")
+        nc.vector.tensor_copy(out=w_f[:], in_=w_bf[:])
+
+        xg = {}
+        x_codes = {}
+        x_scales = {}
+
+        def do_xrg(eng, g):
+            if g not in xg:
+                xg[g] = keep.tile([P, D, 4], BF16, name="xg%d" % g, align_bytes=64)
+            lo, hi = (0, D - XS) if eng == "V" else (D - XS, D)
+            copy_on(
+                eng,
+                xg[g][:, lo:hi, :].rearrange("p (c i) t -> p c t i", i=4),
+                x_sb[g][:, :, lo:hi].rearrange("p t (c i) -> p c t i", i=4),
+            )
+
+        def do_xq(g):
+            x_codes[g] = keep.tile([P, D], U32, name="x_codes%d" % g, align_bytes=64)
+            x_scales[g] = keep.tile([P, D], U8, name="x_scales%d" % g, align_bytes=64)
+            nc.vector.quantize_mx(
+                out=x_codes[g][:].bitcast(FP8X4), scales=x_scales[g][:], in_=xg[g][:].rearrange("p d t -> p (d t)")
+            )
+
+        w0x = {}
+
+        def do_w0x(g, h):
+            t = keep.tile([P, 4, 256], F32, name="w0x%d%d" % (g, h))
+            src = x_sb[g][:, :, 256 * h : 256 * (h + 1)]
+            if W0X_ENG[(g, h)] == "S":
+                nc.scalar.activation(out=t[:], in_=src, func=ACT.Copy, scale=w_f[:, 0:1])
+            elif W0X_ENG[(g, h)] == "V":
+                nc.vector.tensor_scalar(out=t[:], in0=src, scalar1=w_f[:, 0:1], scalar2=None, op0=ALU.mult)
+            else:
+                nc.gpsimd.tensor_scalar(out=t[:], in0=src, scalar1=w_f[:, 0:1], scalar2=0.0, op0=ALU.mult, op1=ALU.add)
+            w0x[(g, h)] = t
+
+        tp = {}
+        ag = {}
+        a_codes = {}
+        a_scales = {}
+
+        def do_T(m):
+            c, e = divmod(m, 2)
+            t = psum.tile([P, 4, P], F32, tag="bank%d" % T_BANK[m], name="tp%d" % m)
+            aw = a_sb[c][:, e, :].bitcast(F32)
+            for k in range(4):
+                nc.tensor.transpose(t[:, k, :], aw[:, 256 * (k // 2) + k % 2 : 256 * (k // 2 + 1) : 2], ident[:])
+            tp[m] = t
+
+        def do_ATc(m):
+            c, e = divmod(m, 2)
+            if c not in ag:
+                ag[c] = keep.tile([P, 2, N], BF16, name="ag%d" % c, align_bytes=64)
+            copy_on(
+                ATC_ENG[m],
+                ag[c][:, e, :].bitcast(F32).rearrange("p (g i u) -> p g i u", g=2, u=2),
+                tp[m][:].rearrange("p (g u) i -> p g i u", u=2),
+            )
+
+        def do_Aq(c):
+            a_codes[c] = keep.tile([P, 512], U32, name="a_codes%d" % c, align_bytes=64)
+            a_scales[c] = keep.tile([P, 512], U8, name="a_scales%d" % c, align_bytes=64)
+            nc.vector.quantize_mx(
+                out=a_codes[c][:].bitcast(FP8X4), scales=a_scales[c][:], in_=ag[c][:].rearrange("p e k -> p (e k)")
+            )
+
+        def lhs(m, gp):
+            c, e = divmod(m, 2)
+            lo = (2 * e + gp) * P
+            return a_codes[c][:, lo : lo + P].bitcast(FP8X4), a_scales[c][:, lo : lo + P]
+
+        hb = {}
+
+        def do_M(m, b):
+            g, t = divmod(m, 4)
+            if (g, b) not in hb:
+                hb[(g, b)] = psum.tile([P, 4, P], F32, tag="bank%d" % H_BANK[(g, b)], name="hb%d%d" % (g, b))
+            for gp in range(2):
+                lt, ls = lhs(m, gp)
+                nc.tensor.matmul_mx(
+                    out=hb[(g, b)][:, t, :],
+                    lhsT=lt,
+                    lhsT_scale=ls,
+                    rhs=x_codes[gp][:, P * b : P * (b + 1)].bitcast(FP8X4),
+                    rhs_scale=x_scales[gp][:, P * b : P * (b + 1)],
+                    start=(gp == 0),
+                    stop=(gp == 1),
+                )
+
+        hg = {}
+        acc = {}
+        h1w = {}
+        h_codes = {}
+        h_scales = {}
+
+        def do_h1c(g, b):
+            h, r = divmod(b, 2)
+            if (g, h) not in hg:
+                hg[(g, h)] = keep.tile([P, 256, 4], BF16, name="hg%d%d" % (g, h), align_bytes=64)
+            copy_on(H1C_ENG[(g, b)], hg[(g, h)][:, P * r : P * (r + 1), :], hb[(g, b)][:].rearrange("p t d -> p d t"))
+
+        def do_h1w(g, b):
+            h1w[(g, b)] = keep.tile([P, 4, P], F32, name="h1w%d%d" % (g, b))
+            nc.scalar.activation(out=h1w[(g, b)][:], in_=hb[(g, b)][:], func=ACT.Copy, scale=w_f[:, 1:2])
+
+        def do_acc(g, b):
+            h, r = divmod(b, 2)
+            if (g, h) not in acc:
+                acc[(g, h)] = keep.tile([P, 4, 256], F32, name="acc%d%d" % (g, h))
+            dst = acc[(g, h)][:, :, P * r : P * (r + 1)]
+            prev = w0x[(g, h)][:, :, P * r : P * (r + 1)]
+            if ACC_PATH[(g, b)] == "V":
+                nc.vector.scalar_tensor_tensor(
+                    out=dst, in0=hb[(g, b)][:], scalar=w_f[:, 1:2], in1=prev, op0=ALU.mult, op1=ALU.add
+                )
+            else:
+                step = 4 // GSPLIT
+                for s in range(0, 4, step):
+                    nc.gpsimd.tensor_tensor(
+                        out=dst[:, s : s + step, :], in0=h1w[(g, b)][:, s : s + step, :], in1=prev[:, s : s + step, :], op=ALU.add
+                    )
+
+        def do_hq(g, h):
+            h_codes[(g, h)] = keep.tile([P, 256], U32, name="h_codes%d%d" % (g, h), align_bytes=64)
+            h_scales[(g, h)] = keep.tile([P, 256], U8, name="h_scales%d%d" % (g, h), align_bytes=64)
+            nc.vector.quantize_mx(
+                out=h_codes[(g, h)][:].bitcast(FP8X4),
+                scales=h_scales[(g, h)][:],
+                in_=hg[(g, h)][:].rearrange("p d t -> p (d t)"),
+            )
+
+        ob = {}
+        h2w = {}
+        o_sb = {}
+
+        def do_O(h, c):
+            ob[(h, c)] = psum.tile([P, 2, 256], F32, tag="bank%d" % O_BANK[(h, c)], name="ob%d%d" % (h, c))
+            for e in range(2):
+                for gp in range(2):
+                    lt, ls = lhs(2 * c + e, gp)
+                    nc.tensor.matmul_mx(
+                        out=ob[(h, c)][:, e, :],
+                        lhsT=lt,
+                        lhsT_scale=ls,
+                        rhs=h_codes[(gp, h)][:].bitcast(FP8X4),
+                        rhs_scale=h_scales[(gp, h)][:],
+                        start=(gp == 0),
+                        stop=(gp == 1),
+                    )
+
+        def do_h2w(h, c):
+            h2w[(h, c)] = keep.tile([P, 2, 256], F32, name="h2w%d%d" % (h, c))
+            nc.scalar.activation(out=h2w[(h, c)][:], in_=ob[(h, c)][:], func=ACT.Copy, scale=w_f[:, 2:3])
+
+        def do_fin(h, c):
+            g, u = divmod(c, 2)
+            o_sb[(h, c)] = keep.tile([P, 2, 256], F32, name="o%d%d" % (h, c))
+            prev = acc[(g, h)][:, 2 * u : 2 * u + 2, :]
+            if FIN_PATH[(h, c)] == "V":
+                nc.vector.scalar_tensor_tensor(
+                    out=o_sb[(h, c)][:], in0=ob[(h, c)][:], scalar=w_f[:, 2:3], in1=prev, op0=ALU.mult, op1=ALU.add
+                )
+            else:
+                step = 2 // min(GSPLIT, 2)
+                for s in range(0, 2, step):
+                    nc.gpsimd.tensor_tensor(
+                        out=o_sb[(h, c)][:, s : s + step, :], in0=h2w[(h, c)][:, s : s + step, :], in1=prev[:, s : s + step, :], op=ALU.add
+                    )
+
+        def do_st(h, c):
+            nc.sync.dma_start(
+                out=out[512 * (c // 2) : 512 * (c // 2 + 1), 256 * h : 256 * (h + 1)].rearrange("(p u e) d -> p u e d", u=2, e=2)[:, c % 2, :, :],
+                in_=o_sb[(h, c)][:],
+            )
+
+        warm = {}
+
+        def do_W(g):
+            if 0 not in warm:
+                warm[0] = psum.tile([P, D], F32, tag="bank%d" % W_BANK, name="warm")
+            nc.tensor.matmul(out=warm[0][:], lhsT=x_sb[g][:, 0, 0:P], rhs=x_sb[g][:, 1, :], start=True, stop=True)
+
+        two = {"w0x": do_w0x, "h1c": do_h1c, "h1w": do_h1w, "acc": do_acc, "fin": do_fin, "h2w": do_h2w}
+        for step_name in ORDER:
+            if step_name[:3] == "xrg":
+                do_xrg(step_name[3], int(step_name[4]))
+            elif step_name[:3] == "ATc":
+                do_ATc(int(step_name[3]))
+            elif step_name[:3] in two:
+                two[step_name[:3]](int(step_name[3]), int(step_name[4]))
+            elif step_name[:2] == "xq":
+                do_xq(int(step_name[2]))
+            elif step_name[:2] == "Aq":
+                do_Aq(int(step_name[2]))
+            elif step_name[:2] == "hq":
+                do_hq(int(step_name[2]), int(step_name[3]))
+            elif step_name[:2] == "st":
+                do_st(int(step_name[2]), int(step_name[3]))
+            elif step_name[0] == "W":
+                do_W(int(step_name[1]))
+            elif step_name[0] == "T":
+                do_T(int(step_name[1]))
+            elif step_name[0] == "M":
+                do_M(int(step_name[1]), int(step_name[3]))
+            else:
+                do_O(int(step_name[1]), int(step_name[2]))

@@ -14,33 +14,8 @@ ACT = mybir.ActivationFunctionType
 P = 128
 N = 1024
 D = 512
+H = D // 2
 FLOPS = 2 * 2 * N * N * D
-
-PIN = True
-XS = 256
-GSPLIT = 1
-ATC_ENG = "SSSSSSSS"
-H1C_ENG = {(1, 0): "S", (1, 1): "V", (1, 2): "S", (1, 3): "V", (0, 0): "S", (0, 1): "S", (0, 2): "S", (0, 3): "S"}
-W0X_ENG = {(1, 0): "V", (1, 1): "V", (0, 0): "V", (0, 1): "V"}
-ACC_PATH = {(1, 0): "G", (1, 1): "G", (1, 2): "G", (1, 3): "G", (0, 0): "V", (0, 1): "V", (0, 2): "V", (0, 3): "G"}
-FIN_PATH = {(1, 0): "V", (1, 1): "V", (1, 2): "V", (1, 3): "V", (0, 0): "V", (0, 1): "V", (0, 2): "V", (0, 3): "V"}
-T_BANK = [4, 5, 6, 7, 4, 5, 6, 7]
-H_BANK = {(1, 0): 4, (1, 1): 5, (1, 2): 6, (1, 3): 7, (0, 0): 0, (0, 1): 1, (0, 2): 2, (0, 3): 3}
-O_BANK = {(1, 0): 2, (1, 1): 3, (1, 2): 6, (1, 3): 7, (0, 0): 0, (0, 1): 1, (0, 2): 4, (0, 3): 5}
-W_BANK = 3
-LOADS = ["x0", "x1", "A0", "A1", "A2", "A3"]
-ORDER = [
-    "w0x01", "xrgV0", "W0", "W0", "W0", "W1", "W1", "T0", "T1", "W1", "xrgS0", "xrgS1",
-    "T2", "ATc0", "xq0", "ATc1", "w0x11", "w0x10", "xrgV1", "xq1", "T3", "W1", "ATc2", "T4",
-    "Aq0", "T5", "W1", "M0b2", "ATc3", "ATc4", "Aq1", "M1b3", "ATc5", "T7", "T6", "M2b2",
-    "M2b3", "M0b3", "M3b3", "ATc7", "w0x00", "Aq2", "ATc6", "M1b2", "Aq3", "M3b2", "h1w03", "acc02",
-    "h1c03", "M1b1", "M4b2", "M2b0", "M5b3", "h1c02", "M5b2", "M4b3", "M6b3", "M7b3", "M0b0", "M7b2",
-    "M6b2", "M1b0", "h1c13", "h1c12", "M3b0", "h1w12", "M5b1", "M3b1", "hq01", "M2b1", "M0b1", "M6b1",
-    "h1c01", "acc03", "acc00", "M7b1", "M4b1", "M7b0", "M6b0", "M5b0", "h1w13", "M4b0", "h1c10", "hq11",
-    "h1c11", "O10", "acc12", "h1c00", "h1w11", "acc01", "acc13", "O11", "O12", "O13", "fin10", "st10",
-    "fin11", "st11", "hq10", "acc11", "hq00", "h1w10", "O00", "fin12", "st12", "acc10", "fin13", "st13",
-    "O01", "fin00", "st00", "O03", "fin01", "st01", "O02", "fin03", "st03", "fin02", "st02",
-]
 
 
 def tile_simpa_pb_kernel(tc, A_p, x_p, w_p, out):
@@ -48,8 +23,7 @@ def tile_simpa_pb_kernel(tc, A_p, x_p, w_p, out):
     with ExitStack() as ctx:
         keep = ctx.enter_context(tc.tile_pool(name="keep", bufs=1))
         psum = ctx.enter_context(tc.psum_pool(name="psum", bufs=1))
-        if PIN:
-            ctx.enter_context(tc.manual_schedule())
+        ctx.enter_context(tc.manual_schedule())
 
         def copy_on(eng, dst, src):
             if eng == "S":
@@ -61,61 +35,80 @@ def tile_simpa_pb_kernel(tc, A_p, x_p, w_p, out):
         nc.scalar.dma_start(out=w_bf[:], in_=w_p.rearrange("a b -> (a b)").partition_broadcast(P))
         x_sb = {}
         a_sb = {}
-        for name in LOADS:
-            i = int(name[1])
-            if name[0] == "x":
-                xt = keep.tile([P, 4, D], BF16, name="x_sb%d" % i)
-                nc.sync.dma_start(
-                    out=xt[:].rearrange("p t d -> p (t d)"),
-                    in_=x_p[512 * i : 512 * (i + 1), :].rearrange("(p t) d -> p (t d)", t=4),
-                )
-                x_sb[i] = xt
-            else:
-                at = keep.tile([P, 2, N], BF16, name="a_sb%d" % i)
-                g, u = divmod(i, 2)
-                nc.sync.dma_start(
-                    out=at[:].rearrange("p e j -> p (e j)"),
-                    in_=A_p[512 * g : 512 * (g + 1), :].rearrange("(p u e) j -> p u (e j)", u=2, e=2)[:, u, :],
-                )
-                a_sb[i] = at
+
+        def load_x(g):
+            x_sb[g] = keep.tile([P, 4, D], BF16, name="x_sb%d" % g)
+            nc.sync.dma_start(
+                out=x_sb[g][:].rearrange("p t d -> p (t d)"),
+                in_=x_p[512 * g : 512 * (g + 1), :].rearrange("(p t) d -> p (t d)", t=4),
+            )
+
+        def load_a(m, count):
+            g, t = divmod(m, 4)
+            rows = A_p[512 * g : 512 * (g + 1), :].rearrange("(p t) j -> p t j", t=4)
+            at = keep.tile([P, count, N], BF16, name="a_sb%d" % m)
+            nc.sync.dma_start(out=at[:], in_=rows[:, t : t + count, :])
+            for i in range(count):
+                a_sb[m + i] = at[:, i, :]
+
+        load_x(0)
+        load_a(0, 2)
+        load_a(2, 2)
+        load_a(4, 2)
+        load_x(1)
+        load_a(6, 1)
+        load_a(7, 1)
+
         ident = keep.tile([P, P], F32, name="ident")
         make_identity(nc, ident[:])
-        w_f = keep.tile([P, 3], F32, name="w_f")
-        nc.vector.tensor_copy(out=w_f[:], in_=w_bf[:])
+        zeros = keep.tile([P, D], BF16, name="zeros")
+        nc.vector.memset(zeros[:], 0.0)
+
+        def do_W(count):
+            for i in range(count):
+                wt = psum.tile([P, D], F32, tag="bank7", name="warm")
+                nc.tensor.matmul(out=wt[:], lhsT=zeros[:, 0:P], rhs=zeros[:], start=True, stop=True)
 
         xg = {}
         x_codes = {}
         x_scales = {}
+        for g in range(2):
+            xg[g] = keep.tile([P, D, 4], BF16, name="xg%d" % g, align_bytes=64)
+            x_codes[g] = keep.tile([P, D], U32, name="x_codes%d" % g, align_bytes=64)
+            x_scales[g] = keep.tile([P, D], U8, name="x_scales%d" % g, align_bytes=64)
 
-        def do_xrg(eng, g):
-            if g not in xg:
-                xg[g] = keep.tile([P, D, 4], BF16, name="xg%d" % g, align_bytes=64)
-            lo, hi = (0, D - XS) if eng == "V" else (D - XS, D)
+        def do_xrg(eng, g, h):
+            lo, hi = H * h, H * (h + 1)
             copy_on(
                 eng,
                 xg[g][:, lo:hi, :].rearrange("p (c i) t -> p c t i", i=4),
                 x_sb[g][:, :, lo:hi].rearrange("p t (c i) -> p c t i", i=4),
             )
 
-        def do_xq(g):
-            x_codes[g] = keep.tile([P, D], U32, name="x_codes%d" % g, align_bytes=64)
-            x_scales[g] = keep.tile([P, D], U8, name="x_scales%d" % g, align_bytes=64)
+        def do_xq(g, h):
+            lo, hi = H * h, H * (h + 1)
             nc.vector.quantize_mx(
-                out=x_codes[g][:].bitcast(FP8X4), scales=x_scales[g][:], in_=xg[g][:].rearrange("p d t -> p (d t)")
+                out=x_codes[g][:, lo:hi].bitcast(FP8X4),
+                scales=x_scales[g][:, lo:hi],
+                in_=xg[g][:, lo:hi, :].rearrange("p d t -> p (d t)"),
             )
 
+        w_f = keep.tile([P, 3], F32, name="w_f")
         w0x = {}
 
-        def do_w0x(g, h):
-            t = keep.tile([P, 4, 256], F32, name="w0x%d%d" % (g, h))
-            src = x_sb[g][:, :, 256 * h : 256 * (h + 1)]
-            if W0X_ENG[(g, h)] == "S":
-                nc.scalar.activation(out=t[:], in_=src, func=ACT.Copy, scale=w_f[:, 0:1])
-            elif W0X_ENG[(g, h)] == "V":
-                nc.vector.tensor_scalar(out=t[:], in0=src, scalar1=w_f[:, 0:1], scalar2=None, op0=ALU.mult)
+        def do_w0x(eng, g, h):
+            w0x[(g, h)] = keep.tile([P, 4, H], F32, name="w0x%d%d" % (g, h))
+            src = x_sb[g][:, :, H * h : H * (h + 1)]
+            if eng == "G":
+                w_g = keep.tile([P, 3], F32, name="w_g")
+                nc.scalar.copy(out=w_g[:], in_=w_f[:])
+                nc.gpsimd.tensor_scalar(
+                    out=w0x[(g, h)][:], in0=src, scalar1=w_g[:, 0:1], scalar2=0.0, op0=ALU.mult, op1=ALU.add
+                )
+            elif eng == "V":
+                nc.vector.tensor_scalar(out=w0x[(g, h)][:], in0=src, scalar1=w_f[:, 0:1], scalar2=None, op0=ALU.mult)
             else:
-                nc.gpsimd.tensor_scalar(out=t[:], in0=src, scalar1=w_f[:, 0:1], scalar2=0.0, op0=ALU.mult, op1=ALU.add)
-            w0x[(g, h)] = t
+                nc.scalar.activation(out=w0x[(g, h)][:], in_=src, func=ACT.Copy, scale=w_f[:, 0:1])
 
         tp = {}
         ag = {}
@@ -123,19 +116,19 @@ def tile_simpa_pb_kernel(tc, A_p, x_p, w_p, out):
         a_scales = {}
 
         def do_T(m):
-            c, e = divmod(m, 2)
-            t = psum.tile([P, 4, P], F32, tag="bank%d" % T_BANK[m], name="tp%d" % m)
-            aw = a_sb[c][:, e, :].bitcast(F32)
+            t = psum.tile([P, 4, P], F32, tag="bank%d" % m, name="tp%d" % m)
+            aw = a_sb[m].bitcast(F32)
             for k in range(4):
-                nc.tensor.transpose(t[:, k, :], aw[:, 256 * (k // 2) + k % 2 : 256 * (k // 2 + 1) : 2], ident[:])
+                g, u = divmod(k, 2)
+                nc.tensor.transpose(t[:, k, :], aw[:, 256 * g + u : 256 * (g + 1) : 2], ident[:])
             tp[m] = t
 
-        def do_ATc(m):
+        def do_AT(eng, m):
             c, e = divmod(m, 2)
             if c not in ag:
                 ag[c] = keep.tile([P, 2, N], BF16, name="ag%d" % c, align_bytes=64)
             copy_on(
-                ATC_ENG[m],
+                eng,
                 ag[c][:, e, :].bitcast(F32).rearrange("p (g i u) -> p g i u", g=2, u=2),
                 tp[m][:].rearrange("p (g u) i -> p g i u", u=2),
             )
@@ -154,21 +147,23 @@ def tile_simpa_pb_kernel(tc, A_p, x_p, w_p, out):
 
         hb = {}
 
-        def do_M(m, b):
+        def do_M(m, h):
             g, t = divmod(m, 4)
-            if (g, b) not in hb:
-                hb[(g, b)] = psum.tile([P, 4, P], F32, tag="bank%d" % H_BANK[(g, b)], name="hb%d%d" % (g, b))
-            for gp in range(2):
-                lt, ls = lhs(m, gp)
-                nc.tensor.matmul_mx(
-                    out=hb[(g, b)][:, t, :],
-                    lhsT=lt,
-                    lhsT_scale=ls,
-                    rhs=x_codes[gp][:, P * b : P * (b + 1)].bitcast(FP8X4),
-                    rhs_scale=x_scales[gp][:, P * b : P * (b + 1)],
-                    start=(gp == 0),
-                    stop=(gp == 1),
-                )
+            for r in range(2):
+                b = 2 * h + r
+                if (g, b) not in hb:
+                    hb[(g, b)] = psum.tile([P, 4, P], F32, tag="bank%d" % (4 * h + 2 * g + r), name="hb%d%d" % (g, b))
+                for gp in range(2):
+                    lt, ls = lhs(m, gp)
+                    nc.tensor.matmul_mx(
+                        out=hb[(g, b)][:, t, :],
+                        lhsT=lt,
+                        lhsT_scale=ls,
+                        rhs=x_codes[gp][:, P * b : P * (b + 1)].bitcast(FP8X4),
+                        rhs_scale=x_scales[gp][:, P * b : P * (b + 1)],
+                        start=(gp == 0),
+                        stop=(gp == 1),
+                    )
 
         hg = {}
         acc = {}
@@ -176,36 +171,33 @@ def tile_simpa_pb_kernel(tc, A_p, x_p, w_p, out):
         h_codes = {}
         h_scales = {}
 
-        def do_h1c(g, b):
+        def do_h1c(eng, g, b):
             h, r = divmod(b, 2)
             if (g, h) not in hg:
-                hg[(g, h)] = keep.tile([P, 256, 4], BF16, name="hg%d%d" % (g, h), align_bytes=64)
-            copy_on(H1C_ENG[(g, b)], hg[(g, h)][:, P * r : P * (r + 1), :], hb[(g, b)][:].rearrange("p t d -> p d t"))
+                hg[(g, h)] = keep.tile([P, H, 4], BF16, name="hg%d%d" % (g, h), align_bytes=64)
+            copy_on(eng, hg[(g, h)][:, P * r : P * (r + 1), :], hb[(g, b)][:].rearrange("p t d -> p d t"))
 
-        def do_h1w(g, b):
-            h1w[(g, b)] = keep.tile([P, 4, P], F32, name="h1w%d%d" % (g, b))
-            nc.scalar.activation(out=h1w[(g, b)][:], in_=hb[(g, b)][:], func=ACT.Copy, scale=w_f[:, 1:2])
-
-        def do_acc(g, b):
+        def acc_parts(g, b):
             h, r = divmod(b, 2)
             if (g, h) not in acc:
-                acc[(g, h)] = keep.tile([P, 4, 256], F32, name="acc%d%d" % (g, h))
-            dst = acc[(g, h)][:, :, P * r : P * (r + 1)]
-            prev = w0x[(g, h)][:, :, P * r : P * (r + 1)]
-            if ACC_PATH[(g, b)] == "V":
-                nc.vector.scalar_tensor_tensor(
-                    out=dst, in0=hb[(g, b)][:], scalar=w_f[:, 1:2], in1=prev, op0=ALU.mult, op1=ALU.add
-                )
-            else:
-                step = 4 // GSPLIT
-                for s in range(0, 4, step):
-                    nc.gpsimd.tensor_tensor(
-                        out=dst[:, s : s + step, :], in0=h1w[(g, b)][:, s : s + step, :], in1=prev[:, s : s + step, :], op=ALU.add
-                    )
+                acc[(g, h)] = keep.tile([P, 4, H], F32, name="acc%d%d" % (g, h))
+            return acc[(g, h)][:, :, P * r : P * (r + 1)], w0x[(g, h)][:, :, P * r : P * (r + 1)]
+
+        def do_acc(g, b):
+            dst, prev = acc_parts(g, b)
+            nc.vector.scalar_tensor_tensor(
+                out=dst, in0=hb[(g, b)][:], scalar=w_f[:, 1:2], in1=prev, op0=ALU.mult, op1=ALU.add
+            )
+
+        def do_accG(g, b):
+            dst, prev = acc_parts(g, b)
+            h1w[(g, b)] = keep.tile([P, 4, P], F32, name="h1w%d%d" % (g, b))
+            nc.scalar.activation(out=h1w[(g, b)][:], in_=hb[(g, b)][:], func=ACT.Copy, scale=w_f[:, 1:2])
+            nc.gpsimd.tensor_tensor(out=dst, in0=h1w[(g, b)][:], in1=prev, op=ALU.add)
 
         def do_hq(g, h):
-            h_codes[(g, h)] = keep.tile([P, 256], U32, name="h_codes%d%d" % (g, h), align_bytes=64)
-            h_scales[(g, h)] = keep.tile([P, 256], U8, name="h_scales%d%d" % (g, h), align_bytes=64)
+            h_codes[(g, h)] = keep.tile([P, H], U32, name="h_codes%d%d" % (g, h), align_bytes=64)
+            h_scales[(g, h)] = keep.tile([P, H], U8, name="h_scales%d%d" % (g, h), align_bytes=64)
             nc.vector.quantize_mx(
                 out=h_codes[(g, h)][:].bitcast(FP8X4),
                 scales=h_scales[(g, h)][:],
@@ -213,11 +205,10 @@ def tile_simpa_pb_kernel(tc, A_p, x_p, w_p, out):
             )
 
         ob = {}
-        h2w = {}
         o_sb = {}
 
         def do_O(h, c):
-            ob[(h, c)] = psum.tile([P, 2, 256], F32, tag="bank%d" % O_BANK[(h, c)], name="ob%d%d" % (h, c))
+            ob[(h, c)] = psum.tile([P, 2, H], F32, tag="bank%d" % (4 * h + c), name="ob%d%d" % (h, c))
             for e in range(2):
                 for gp in range(2):
                     lt, ls = lhs(2 * c + e, gp)
@@ -231,59 +222,100 @@ def tile_simpa_pb_kernel(tc, A_p, x_p, w_p, out):
                         stop=(gp == 1),
                     )
 
-        def do_h2w(h, c):
-            h2w[(h, c)] = keep.tile([P, 2, 256], F32, name="h2w%d%d" % (h, c))
-            nc.scalar.activation(out=h2w[(h, c)][:], in_=ob[(h, c)][:], func=ACT.Copy, scale=w_f[:, 2:3])
-
-        def do_fin(h, c):
+        def do_fin(path, h, c):
             g, u = divmod(c, 2)
-            o_sb[(h, c)] = keep.tile([P, 2, 256], F32, name="o%d%d" % (h, c))
+            o = keep.tile([P, 2, H], F32, name="o%d%d" % (h, c))
             prev = acc[(g, h)][:, 2 * u : 2 * u + 2, :]
-            if FIN_PATH[(h, c)] == "V":
+            if path == "V":
                 nc.vector.scalar_tensor_tensor(
-                    out=o_sb[(h, c)][:], in0=ob[(h, c)][:], scalar=w_f[:, 2:3], in1=prev, op0=ALU.mult, op1=ALU.add
+                    out=o[:], in0=ob[(h, c)][:], scalar=w_f[:, 2:3], in1=prev, op0=ALU.mult, op1=ALU.add
                 )
             else:
-                step = 2 // min(GSPLIT, 2)
-                for s in range(0, 2, step):
-                    nc.gpsimd.tensor_tensor(
-                        out=o_sb[(h, c)][:, s : s + step, :], in0=h2w[(h, c)][:, s : s + step, :], in1=prev[:, s : s + step, :], op=ALU.add
-                    )
+                h2w = keep.tile([P, 2, H], F32, name="h2w%d%d" % (h, c))
+                nc.scalar.activation(out=h2w[:], in_=ob[(h, c)][:], func=ACT.Copy, scale=w_f[:, 2:3])
+                nc.gpsimd.tensor_tensor(out=o[:], in0=h2w[:], in1=prev, op=ALU.add)
+            o_sb[(h, c)] = o
 
         def do_st(h, c):
-            nc.sync.dma_start(
-                out=out[512 * (c // 2) : 512 * (c // 2 + 1), 256 * h : 256 * (h + 1)].rearrange("(p u e) d -> p u e d", u=2, e=2)[:, c % 2, :, :],
-                in_=o_sb[(h, c)][:],
-            )
+            g, u = divmod(c, 2)
+            rows = out[512 * g : 512 * (g + 1), H * h : H * (h + 1)].rearrange("(p t) d -> p t d", t=4)
+            nc.sync.dma_start(out=rows[:, 2 * u : 2 * u + 2, :], in_=o_sb[(h, c)][:])
 
-        warm = {}
+        do_W(7)
+        do_xrg("V", 0, 0)
+        do_xrg("S", 0, 1)
+        nc.vector.tensor_copy(out=w_f[:], in_=w_bf[:])
+        do_w0x("V", 0, 0)
+        do_xq(0, 0)
+        do_T(0)
+        do_T(1)
+        do_AT("S", 0)
+        do_AT("S", 1)
+        do_xq(0, 1)
+        do_w0x("V", 0, 1)
+        do_T(2)
+        do_T(3)
+        do_AT("S", 2)
+        do_AT("S", 3)
+        do_Aq(0)
+        do_W(2)
+        do_T(4)
+        do_T(5)
+        do_AT("S", 4)
+        do_AT("S", 5)
+        do_Aq(1)
+        do_xrg("V", 1, 0)
+        do_T(6)
+        do_T(7)
+        do_AT("S", 6)
+        do_AT("S", 7)
+        do_xq(1, 0)
+        do_xrg("V", 1, 1)
+        do_Aq(2)
+        do_Aq(3)
+        do_xq(1, 1)
+        do_w0x("S", 1, 0)
 
-        def do_W(g):
-            if 0 not in warm:
-                warm[0] = psum.tile([P, D], F32, tag="bank%d" % W_BANK, name="warm")
-            nc.tensor.matmul(out=warm[0][:], lhsT=x_sb[g][:, 0, 0:P], rhs=x_sb[g][:, 1, :], start=True, stop=True)
-
-        two = {"w0x": do_w0x, "h1c": do_h1c, "h1w": do_h1w, "acc": do_acc, "fin": do_fin, "h2w": do_h2w}
-        for step_name in ORDER:
-            if step_name[:3] == "xrg":
-                do_xrg(step_name[3], int(step_name[4]))
-            elif step_name[:3] == "ATc":
-                do_ATc(int(step_name[3]))
-            elif step_name[:3] in two:
-                two[step_name[:3]](int(step_name[3]), int(step_name[4]))
-            elif step_name[:2] == "xq":
-                do_xq(int(step_name[2]))
-            elif step_name[:2] == "Aq":
-                do_Aq(int(step_name[2]))
-            elif step_name[:2] == "hq":
-                do_hq(int(step_name[2]), int(step_name[3]))
-            elif step_name[:2] == "st":
-                do_st(int(step_name[2]), int(step_name[3]))
-            elif step_name[0] == "W":
-                do_W(int(step_name[1]))
-            elif step_name[0] == "T":
-                do_T(int(step_name[1]))
-            elif step_name[0] == "M":
-                do_M(int(step_name[1]), int(step_name[3]))
-            else:
-                do_O(int(step_name[1]), int(step_name[2]))
+        for m in range(4):
+            do_M(m, 0)
+        do_w0x("G", 1, 1)
+        do_h1c("S", 0, 0)
+        do_h1c("S", 0, 1)
+        do_acc(0, 0)
+        do_acc(0, 1)
+        do_hq(0, 0)
+        for m in range(4, 8):
+            do_M(m, 0)
+        do_h1c("S", 1, 0)
+        do_h1c("V", 1, 1)
+        do_accG(1, 1)
+        do_acc(1, 0)
+        do_hq(1, 0)
+        for m in range(4):
+            do_M(m, 1)
+        do_h1c("S", 0, 2)
+        do_h1c("S", 0, 3)
+        do_acc(0, 2)
+        do_acc(0, 3)
+        for m in range(4, 8):
+            do_M(m, 1)
+        for c in range(4):
+            do_O(0, c)
+        do_h1c("S", 1, 2)
+        do_h1c("S", 1, 3)
+        do_fin("V", 0, 0)
+        do_hq(0, 1)
+        do_hq(1, 1)
+        do_accG(1, 2)
+        do_accG(1, 3)
+        do_fin("V", 0, 1)
+        do_fin("V", 0, 2)
+        do_fin("G", 0, 3)
+        for c in range(4):
+            do_O(1, c)
+        do_fin("V", 1, 0)
+        do_fin("V", 1, 1)
+        do_fin("V", 1, 2)
+        do_fin("V", 1, 3)
+        for h, c in ((0, 0), (0, 1), (0, 2), (1, 0), (1, 1), (1, 2), (0, 3), (1, 3)):
+            do_st(h, c)

@@ -64,10 +64,11 @@ def tile_simpa_pb_kernel(tc, A_p, x_p, w_p, out):
         zeros = keep.tile([P, D], BF16, name="zeros")
         nc.vector.memset(zeros[:], 0.0)
 
+        warm = psum.tile([P, D], F32, tag="bank7", name="warm")
+
         def do_W(count):
             for i in range(count):
-                wt = psum.tile([P, D], F32, tag="bank7", name="warm")
-                nc.tensor.matmul(out=wt[:], lhsT=zeros[:, 0:P], rhs=zeros[:], start=True, stop=True)
+                nc.tensor.matmul(out=warm[:], lhsT=zeros[:, 0:P], rhs=zeros[:], start=True, stop=True)
 
         xg = {}
         x_codes = {}
@@ -99,13 +100,7 @@ def tile_simpa_pb_kernel(tc, A_p, x_p, w_p, out):
         def do_w0x(eng, g, h):
             w0x[(g, h)] = keep.tile([P, 4, H], F32, name="w0x%d%d" % (g, h))
             src = x_sb[g][:, :, H * h : H * (h + 1)]
-            if eng == "G":
-                w_g = keep.tile([P, 3], F32, name="w_g")
-                nc.scalar.copy(out=w_g[:], in_=w_f[:])
-                nc.gpsimd.tensor_scalar(
-                    out=w0x[(g, h)][:], in0=src, scalar1=w_g[:, 0:1], scalar2=0.0, op0=ALU.mult, op1=ALU.add
-                )
-            elif eng == "V":
+            if eng == "V":
                 nc.vector.tensor_scalar(out=w0x[(g, h)][:], in0=src, scalar1=w_f[:, 0:1], scalar2=None, op0=ALU.mult)
             else:
                 nc.scalar.activation(out=w0x[(g, h)][:], in_=src, func=ACT.Copy, scale=w_f[:, 0:1])
@@ -278,25 +273,24 @@ def tile_simpa_pb_kernel(tc, A_p, x_p, w_p, out):
 
         for m in range(4):
             do_M(m, 0)
-        do_w0x("G", 1, 1)
         do_h1c("S", 0, 0)
         do_h1c("S", 0, 1)
+        do_w0x("V", 1, 1)
         do_acc(0, 0)
-        do_acc(0, 1)
-        do_hq(0, 0)
+        do_accG(0, 1)
         for m in range(4, 8):
             do_M(m, 0)
         do_h1c("S", 1, 0)
         do_h1c("V", 1, 1)
-        do_accG(1, 1)
-        do_acc(1, 0)
+        do_hq(0, 0)
+        do_acc(1, 1)
         do_hq(1, 0)
+        do_acc(1, 0)
         for m in range(4):
             do_M(m, 1)
         do_h1c("S", 0, 2)
         do_h1c("S", 0, 3)
         do_acc(0, 2)
-        do_acc(0, 3)
         for m in range(4, 8):
             do_M(m, 1)
         for c in range(4):
@@ -306,11 +300,12 @@ def tile_simpa_pb_kernel(tc, A_p, x_p, w_p, out):
         do_fin("V", 0, 0)
         do_hq(0, 1)
         do_hq(1, 1)
+        do_accG(0, 3)
         do_accG(1, 2)
-        do_accG(1, 3)
         do_fin("V", 0, 1)
         do_fin("V", 0, 2)
         do_fin("G", 0, 3)
+        do_acc(1, 3)
         for c in range(4):
             do_O(1, c)
         do_fin("V", 1, 0)

@@ -54,15 +54,15 @@ def tile_simpa_pb_kernel(tc, A_p, x_p, w_p, out):
         load_x(0)
         load_a(0, 2)
         load_a(2, 2)
-        load_a(4, 2)
         load_x(1)
+        load_a(4, 2)
         load_a(6, 1)
         load_a(7, 1)
 
         ident = keep.tile([P, P], F32, name="ident")
         make_identity(nc, ident[:])
         zeros = keep.tile([P, D], BF16, name="zeros")
-        nc.vector.memset(zeros[:], 0.0)
+        nc.gpsimd.memset(zeros[:], 0.0)
 
         warm = psum.tile([P, D], F32, tag="bank7", name="warm")
 
@@ -236,7 +236,7 @@ def tile_simpa_pb_kernel(tc, A_p, x_p, w_p, out):
             rows = out[512 * g : 512 * (g + 1), H * h : H * (h + 1)].rearrange("(p t) d -> p t d", t=4)
             nc.sync.dma_start(out=rows[:, 2 * u : 2 * u + 2, :], in_=o_sb[(h, c)][:])
 
-        do_W(7)
+        do_W(6)
         do_xrg("V", 0, 0)
         do_xrg("S", 0, 1)
         nc.vector.tensor_copy(out=w_f[:], in_=w_bf[:])
@@ -248,64 +248,65 @@ def tile_simpa_pb_kernel(tc, A_p, x_p, w_p, out):
         do_AT("S", 1)
         do_xq(0, 1)
         do_w0x("V", 0, 1)
+        do_W(2)
         do_T(2)
         do_T(3)
         do_AT("S", 2)
         do_AT("S", 3)
         do_Aq(0)
+        do_xrg("V", 1, 0)
         do_W(2)
+        do_Aq(1)
+        do_xq(1, 0)
         do_T(4)
         do_T(5)
         do_AT("S", 4)
         do_AT("S", 5)
-        do_Aq(1)
-        do_xrg("V", 1, 0)
+        do_xrg("V", 1, 1)
+        do_w0x("V", 1, 0)
         do_T(6)
         do_T(7)
         do_AT("S", 6)
         do_AT("S", 7)
-        do_xq(1, 0)
-        do_xrg("V", 1, 1)
         do_Aq(2)
-        do_Aq(3)
         do_xq(1, 1)
-        do_w0x("S", 1, 0)
+        do_Aq(3)
+        do_w0x("S", 1, 1)
 
         for m in range(4):
             do_M(m, 0)
-        do_h1c("S", 0, 0)
+        do_h1c("V", 0, 0)
         do_h1c("S", 0, 1)
-        do_w0x("V", 1, 1)
         do_acc(0, 0)
-        do_accG(0, 1)
+        do_hq(0, 0)
+        do_acc(0, 1)
         for m in range(4, 8):
             do_M(m, 0)
         do_h1c("S", 1, 0)
-        do_h1c("V", 1, 1)
-        do_hq(0, 0)
-        do_acc(1, 1)
-        do_hq(1, 0)
+        do_h1c("S", 1, 1)
         do_acc(1, 0)
+        do_hq(1, 0)
+        do_acc(1, 1)
         for m in range(4):
             do_M(m, 1)
         do_h1c("S", 0, 2)
         do_h1c("S", 0, 3)
         do_acc(0, 2)
+        do_acc(0, 3)
         for m in range(4, 8):
             do_M(m, 1)
         for c in range(4):
             do_O(0, c)
         do_h1c("S", 1, 2)
         do_h1c("S", 1, 3)
-        do_fin("V", 0, 0)
         do_hq(0, 1)
         do_hq(1, 1)
-        do_accG(0, 3)
+        do_fin("V", 0, 0)
         do_accG(1, 2)
+        do_accG(1, 3)
         do_fin("V", 0, 1)
         do_fin("V", 0, 2)
         do_fin("G", 0, 3)
-        do_acc(1, 3)
         for c in range(4):
             do_O(1, c)
         do_fin("V", 1, 0)

@@ -142,14 +142,11 @@ def tile_simpa_pb_kernel(tc, A_p, x_p, w_p, out):
 
         hb = {}
 
-        def do_M(m, h):
-            g, t = divmod(m, 4)
-            for r in range(2):
-                b = 2 * h + r
-                if (g, b) not in hb:
-                    hb[(g, b)] = psum.tile([P, 4, P], F32, tag="bank%d" % (4 * h + 2 * g + r), name="hb%d%d" % (g, b))
+        def do_M(g, b):
+            hb[(g, b)] = psum.tile([P, 4, P], F32, tag="bank%d" % (4 * g + b), name="hb%d%d" % (g, b))
+            for t in range(4):
                 for gp in range(2):
-                    lt, ls = lhs(m, gp)
+                    lt, ls = lhs(4 * g + t, gp)
                     nc.tensor.matmul_mx(
                         out=hb[(g, b)][:, t, :],
                         lhsT=lt,
@@ -258,60 +255,42 @@ def tile_simpa_pb_kernel(tc, A_p, x_p, w_p, out):
         do_W(2)
         do_Aq(1)
         do_xq(1, 0)
+        do_w0x("S", 1, 0)
         do_T(4)
         do_T(5)
         do_AT("S", 4)
         do_AT("S", 5)
         do_xrg("V", 1, 1)
-        do_w0x("V", 1, 0)
+        do_w0x("V", 1, 1)
+        do_xq(1, 1)
+        do_W(1)
         do_T(6)
         do_T(7)
         do_AT("S", 6)
         do_AT("S", 7)
         do_Aq(2)
-        do_xq(1, 1)
         do_Aq(3)
-        do_w0x("S", 1, 1)
 
-        for m in range(4):
-            do_M(m, 0)
-        do_h1c("V", 0, 0)
-        do_h1c("S", 0, 1)
+        for b in range(4):
+            do_M(0, b)
+            do_h1c("S", 0, b)
         do_acc(0, 0)
-        do_hq(0, 0)
         do_acc(0, 1)
-        for m in range(4, 8):
-            do_M(m, 0)
-        do_h1c("S", 1, 0)
-        do_h1c("S", 1, 1)
-        do_acc(1, 0)
-        do_hq(1, 0)
-        do_acc(1, 1)
-        for m in range(4):
-            do_M(m, 1)
-        do_h1c("S", 0, 2)
-        do_h1c("S", 0, 3)
+        do_hq(0, 0)
         do_acc(0, 2)
         do_acc(0, 3)
-        for m in range(4, 8):
-            do_M(m, 1)
-        for c in range(4):
-            do_O(0, c)
-        do_h1c("S", 1, 2)
-        do_h1c("S", 1, 3)
         do_hq(0, 1)
+        for b in range(4):
+            do_M(1, b)
+            do_h1c("S", 1, b)
+        do_hq(1, 0)
+        do_acc(1, 0)
+        do_acc(1, 1)
         do_hq(1, 1)
-        do_fin("V", 0, 0)
         do_accG(1, 2)
         do_accG(1, 3)
-        do_fin("V", 0, 1)
-        do_fin("V", 0, 2)
-        do_fin("G", 0, 3)
-        for c in range(4):
-            do_O(1, c)
-        do_fin("V", 1, 0)
-        do_fin("V", 1, 1)
-        do_fin("V", 1, 2)
-        do_fin("V", 1, 3)
-        for h, c in ((0, 0), (0, 1), (0, 2), (1, 0), (1, 1), (1, 2), (0, 3), (1, 3)):
-            do_st(h, c)
+        for h in range(2):
+            for c in range(4):
+                do_O(h, c)
+                do_fin("V", h, c)
+                do_st(h, c)

@@ -282,15 +282,24 @@ def tile_simpa_pb_kernel(tc, A_p, x_p, w_p, out):
         do_hq(0, 1)
         for b in range(4):
             do_M(1, b)
-            do_h1c("S", 1, b)
+        do_h1c("S", 1, 0)
+        do_h1c("S", 1, 1)
+        do_accG(1, 1)
         do_hq(1, 0)
         do_acc(1, 0)
-        do_acc(1, 1)
+        do_h1c("S", 1, 2)
+        do_h1c("S", 1, 3)
+        do_O(0, 0)
+        do_fin("V", 0, 0)
         do_hq(1, 1)
         do_accG(1, 2)
         do_accG(1, 3)
+        for c in range(1, 4):
+            do_O(0, c)
+            do_fin("V", 0, c)
+        for c in range(4):
+            do_O(1, c)
+            do_fin("V", 1, c)
         for h in range(2):
             for c in range(4):
-                do_O(h, c)
-                do_fin("V", h, c)
                 do_st(h, c)

@@ -54,8 +54,8 @@ def tile_simpa_pb_kernel(tc, A_p, x_p, w_p, out):
         load_x(0)
         load_a(0, 2)
         load_a(2, 2)
-        load_x(1)
         load_a(4, 2)
+        load_x(1)
         load_a(6, 1)
         load_a(7, 1)
 
@@ -95,12 +95,17 @@ def tile_simpa_pb_kernel(tc, A_p, x_p, w_p, out):
             )
 
         w_f = keep.tile([P, 3], F32, name="w_f")
+        w_g = keep.tile([P, 3], F32, name="w_g")
         w0x = {}
 
         def do_w0x(eng, g, h):
             w0x[(g, h)] = keep.tile([P, 4, H], F32, name="w0x%d%d" % (g, h))
             src = x_sb[g][:, :, H * h : H * (h + 1)]
-            if eng == "V":
+            if eng == "G":
+                nc.gpsimd.tensor_scalar(
+                    out=w0x[(g, h)][:], in0=src, scalar1=w_g[:, 0:1], scalar2=0.0, op0=ALU.mult, op1=ALU.add
+                )
+            elif eng == "V":
                 nc.vector.tensor_scalar(out=w0x[(g, h)][:], in0=src, scalar1=w_f[:, 0:1], scalar2=None, op0=ALU.mult)
             else:
                 nc.scalar.activation(out=w0x[(g, h)][:], in_=src, func=ACT.Copy, scale=w_f[:, 0:1])
@@ -200,7 +205,7 @@ def tile_simpa_pb_kernel(tc, A_p, x_p, w_p, out):
         o_sb = {}
 
         def do_O(h, c):
-            ob[(h, c)] = psum.tile([P, 2, H], F32, tag="bank%d" % (4 * h + c), name="ob%d%d" % (h, c))
+            ob[(h, c)] = psum.tile([P, 2, H], F32, tag="bank%d" % len(ob), name="ob%d%d" % (h, c))
             for e in range(2):
                 for gp in range(2):
                     lt, ls = lhs(2 * c + e, gp)
@@ -216,24 +221,25 @@ def tile_simpa_pb_kernel(tc, A_p, x_p, w_p, out):
 
         def do_fin(path, h, c):
             g, u = divmod(c, 2)
-            o = keep.tile([P, 2, H], F32, name="o%d%d" % (h, c))
+            if c not in o_sb:
+                o_sb[c] = keep.tile([P, 2, D], F32, name="o%d" % c)
+            o = o_sb[c][:, :, H * h : H * (h + 1)]
             prev = acc[(g, h)][:, 2 * u : 2 * u + 2, :]
             if path == "V":
                 nc.vector.scalar_tensor_tensor(
-                    out=o[:], in0=ob[(h, c)][:], scalar=w_f[:, 2:3], in1=prev, op0=ALU.mult, op1=ALU.add
+                    out=o, in0=ob[(h, c)][:], scalar=w_f[:, 2:3], in1=prev, op0=ALU.mult, op1=ALU.add
                 )
             else:
                 h2w = keep.tile([P, 2, H], F32, name="h2w%d%d" % (h, c))
                 nc.scalar.activation(out=h2w[:], in_=ob[(h, c)][:], func=ACT.Copy, scale=w_f[:, 2:3])
-                nc.gpsimd.tensor_tensor(out=o[:], in0=h2w[:], in1=prev, op=ALU.add)
-            o_sb[(h, c)] = o
+                nc.gpsimd.tensor_tensor(out=o, in0=h2w[:], in1=prev, op=ALU.add)
 
-        def do_st(h, c):
+        def do_st(c, lo, hi):
             g, u = divmod(c, 2)
-            rows = out[512 * g : 512 * (g + 1), H * h : H * (h + 1)].rearrange("(p t) d -> p t d", t=4)
-            nc.sync.dma_start(out=rows[:, 2 * u : 2 * u + 2, :], in_=o_sb[(h, c)][:])
+            rows = out[512 * g : 512 * (g + 1), lo:hi].rearrange("(p t) d -> p t d", t=4)
+            nc.sync.dma_start(out=rows[:, 2 * u : 2 * u + 2, :], in_=o_sb[c][:, :, lo:hi])
 
-        do_W(6)
+        do_W(7)
         do_xrg("V", 0, 0)
         do_xrg("S", 0, 1)
         nc.vector.tensor_copy(out=w_f[:], in_=w_bf[:])
@@ -251,25 +257,25 @@ def tile_simpa_pb_kernel(tc, A_p, x_p, w_p, out):
         do_AT("S", 2)
         do_AT("S", 3)
         do_Aq(0)
-        do_xrg("V", 1, 0)
-        do_W(2)
-        do_Aq(1)
-        do_xq(1, 0)
-        do_w0x("S", 1, 0)
         do_T(4)
         do_T(5)
         do_AT("S", 4)
         do_AT("S", 5)
+        do_xrg("V", 1, 0)
+        do_Aq(1)
+        do_xq(1, 0)
         do_xrg("V", 1, 1)
-        do_w0x("V", 1, 1)
-        do_xq(1, 1)
-        do_W(1)
+        do_W(2)
         do_T(6)
         do_T(7)
         do_AT("S", 6)
         do_AT("S", 7)
         do_Aq(2)
+        do_xq(1, 1)
         do_Aq(3)
+        nc.vector.tensor_copy(out=w_g[:], in_=w_f[:])
+        do_w0x("G", 1, 0)
+        do_w0x("G", 1, 1)
 
         for b in range(4):
             do_M(0, b)
@@ -279,27 +285,40 @@ def tile_simpa_pb_kernel(tc, A_p, x_p, w_p, out):
         do_hq(0, 0)
         do_acc(0, 2)
         do_acc(0, 3)
-        do_hq(0, 1)
         for b in range(4):
             do_M(1, b)
         do_h1c("S", 1, 0)
         do_h1c("S", 1, 1)
         do_accG(1, 1)
         do_hq(1, 0)
+        do_hq(0, 1)
         do_acc(1, 0)
         do_h1c("S", 1, 2)
         do_h1c("S", 1, 3)
         do_O(0, 0)
         do_fin("V", 0, 0)
+        do_st(0, 0, H)
         do_hq(1, 1)
         do_accG(1, 2)
         do_accG(1, 3)
-        for c in range(1, 4):
-            do_O(0, c)
-            do_fin("V", 0, c)
-        for c in range(4):
-            do_O(1, c)
-            do_fin("V", 1, c)
-        for h in range(2):
-            for c in range(4):
-                do_st(h, c)
+        do_O(0, 1)
+        do_fin("V", 0, 1)
+        do_st(1, 0, H)
+        do_O(0, 2)
+        do_fin("V", 0, 2)
+        do_st(2, 0, H)
+        do_O(0, 3)
+        do_fin("V", 0, 3)
+        do_st(3, 0, H)
+        do_O(1, 0)
+        do_fin("V", 1, 0)
+        do_st(0, H, D)
+        do_O(1, 1)
+        do_fin("V", 1, 1)
+        do_st(1, H, D)
+        do_O(1, 2)
+        do_fin("V", 1, 2)
+        do_st(2, H, D)
+        do_O(1, 3)
+        do_fin("V", 1, 3)
+        do_st(3, H, D)

from contextlib import ExitStack

import concourse.mybir as mybir
from concourse.masks import make_identity

F32 = mybir.dt.float32
BF16 = mybir.dt.bfloat16
U32 = mybir.dt.uint32
U8 = mybir.dt.uint8
FP8X4 = mybir.dt.float8_e4m3fn_x4
ALU = mybir.AluOpType
ACT = mybir.ActivationFunctionType

P = 128
N = 1024
D = 512
H = D // 2
FLOPS = 2 * 2 * N * N * D


def tile_simpa_pb_kernel(tc, A_p, x_p, w_p, out):
    nc = tc.nc
    with ExitStack() as ctx:
        keep = ctx.enter_context(tc.tile_pool(name="keep", bufs=1))
        psum = ctx.enter_context(tc.psum_pool(name="psum", bufs=1))
        ctx.enter_context(tc.manual_schedule())

        def copy_on(eng, dst, src):
            if eng == "S":
                nc.scalar.copy(out=dst, in_=src)
            else:
                nc.vector.tensor_copy(out=dst, in_=src)

        w_bf = keep.tile([P, 3], BF16, name="w_bf")
        nc.scalar.dma_start(out=w_bf[:], in_=w_p.rearrange("a b -> (a b)").partition_broadcast(P))
        x_sb = {}
        a_sb = {}

        def load_x(g):
            x_sb[g] = keep.tile([P, 4, D], BF16, name="x_sb%d" % g)
            nc.sync.dma_start(
                out=x_sb[g][:].rearrange("p t d -> p (t d)"),
                in_=x_p[512 * g : 512 * (g + 1), :].rearrange("(p t) d -> p (t d)", t=4),
            )

        def load_a(m, count):
            g, t = divmod(m, 4)
            rows = A_p[512 * g : 512 * (g + 1), :].rearrange("(p t) j -> p t j", t=4)
            at = keep.tile([P, count, N], BF16, name="a_sb%d" % m)
            nc.sync.dma_start(out=at[:], in_=rows[:, t : t + count, :])
            for i in range(count):
                a_sb[m + i] = at[:, i, :]

        load_x(0)
        load_a(0, 2)
        load_a(2, 2)
        load_a(4, 2)
        load_x(1)
        load_a(6, 1)
        load_a(7, 1)

        ident = keep.tile([P, P], F32, name="ident")
        make_identity(nc, ident[:])
        zeros = keep.tile([P, D], BF16, name="zeros")
        nc.gpsimd.memset(zeros[:], 0.0)

        warm = psum.tile([P, D], F32, tag="bank7", name="warm")

        def do_W(count):
            for i in range(count):
                nc.tensor.matmul(out=warm[:], lhsT=zeros[:, 0:P], rhs=zeros[:], start=True, stop=True)

        xg = {}
        x_codes = {}
        x_scales = {}
        for g in range(2):
            xg[g] = keep.tile([P, D, 4], BF16, name="xg%d" % g, align_bytes=64)
            x_codes[g] = keep.tile([P, D], U32, name="x_codes%d" % g, align_bytes=64)
            x_scales[g] = keep.tile([P, D], U8, name="x_scales%d" % g, align_bytes=64)

        def do_xrg(eng, g, h):
            lo, hi = H * h, H * (h + 1)
            copy_on(
                eng,
                xg[g][:, lo:hi, :].rearrange("p (c i) t -> p c t i", i=4),
                x_sb[g][:, :, lo:hi].rearrange("p t (c i) -> p c t i", i=4),
            )

        def do_xq(g, h):
            lo, hi = H * h, H * (h + 1)
            nc.vector.quantize_mx(
                out=x_codes[g][:, lo:hi].bitcast(FP8X4),
                scales=x_scales[g][:, lo:hi],
                in_=xg[g][:, lo:hi, :].rearrange("p d t -> p (d t)"),
            )

        w_f = keep.tile([P, 3], F32, name="w_f")
        w_g = keep.tile([P, 3], F32, name="w_g")
        w0x = {}

        def do_w0x(eng, g, h):
            w0x[(g, h)] = keep.tile([P, 4, H], F32, name="w0x%d%d" % (g, h))
            src = x_sb[g][:, :, H * h : H * (h + 1)]
            if eng == "G":
                nc.gpsimd.tensor_scalar(
                    out=w0x[(g, h)][:], in0=src, scalar1=w_g[:, 0:1], scalar2=0.0, op0=ALU.mult, op1=ALU.add
                )
            elif eng == "V":
                nc.vector.tensor_scalar(out=w0x[(g, h)][:], in0=src, scalar1=w_f[:, 0:1], scalar2=None, op0=ALU.mult)
            else:
                nc.scalar.activation(out=w0x[(g, h)][:], in_=src, func=ACT.Copy, scale=w_f[:, 0:1])

        tp = {}
        ag = {}
        a_codes = {}
        a_scales = {}

        def do_T(m):
            t = psum.tile([P, 4, P], F32, tag="bank%d" % m, name="tp%d" % m)
            aw = a_sb[m].bitcast(F32)
            for k in range(4):
                g, u = divmod(k, 2)
                nc.tensor.transpose(t[:, k, :], aw[:, 256 * g + u : 256 * (g + 1) : 2], ident[:])
            tp[m] = t

        def do_AT(eng, m):
            c, e = divmod(m, 2)
            if c not in ag:
                ag[c] = keep.tile([P, 2, N], BF16, name="ag%d" % c, align_bytes=64)
            copy_on(
                eng,
                ag[c][:, e, :].bitcast(F32).rearrange("p (g i u) -> p g i u", g=2, u=2),
                tp[m][:].rearrange("p (g u) i -> p g i u", u=2),
            )

        def do_Aq(c):
            a_codes[c] = keep.tile([P, 512], U32, name="a_codes%d" % c, align_bytes=64)
            a_scales[c] = keep.tile([P, 512], U8, name="a_scales%d" % c, align_bytes=64)
            nc.vector.quantize_mx(
                out=a_codes[c][:].bitcast(FP8X4), scales=a_scales[c][:], in_=ag[c][:].rearrange("p e k -> p (e k)")
            )

        def lhs(m, gp):
            c, e = divmod(m, 2)
            lo = (2 * e + gp) * P
            return a_codes[c][:, lo : lo + P].bitcast(FP8X4), a_scales[c][:, lo : lo + P]

        hb = {}

        def do_M(g, b):
            hb[(g, b)] = psum.tile([P, 4, P], F32, tag="bank%d" % (4 * g + b), name="hb%d%d" % (g, b))
            for t in range(4):
                for gp in range(2):
                    lt, ls = lhs(4 * g + t, gp)
                    nc.tensor.matmul_mx(
                        out=hb[(g, b)][:, t, :],
                        lhsT=lt,
                        lhsT_scale=ls,
                        rhs=x_codes[gp][:, P * b : P * (b + 1)].bitcast(FP8X4),
                        rhs_scale=x_scales[gp][:, P * b : P * (b + 1)],
                        start=(gp == 0),
                        stop=(gp == 1),
                    )

        hg = {}
        acc = {}
        h1w = {}
        h_codes = {}
        h_scales = {}

        def do_h1c(eng, g, b):
            h, r = divmod(b, 2)
            if (g, h) not in hg:
                hg[(g, h)] = keep.tile([P, H, 4], BF16, name="hg%d%d" % (g, h), align_bytes=64)
            copy_on(eng, hg[(g, h)][:, P * r : P * (r + 1), :], hb[(g, b)][:].rearrange("p t d -> p d t"))

        def acc_parts(g, b):
            h, r = divmod(b, 2)
            if (g, h) not in acc:
                acc[(g, h)] = keep.tile([P, 4, H], F32, name="acc%d%d" % (g, h))
            return acc[(g, h)][:, :, P * r : P * (r + 1)], w0x[(g, h)][:, :, P * r : P * (r + 1)]

        def do_acc(g, b):
            dst, prev = acc_parts(g, b)
            nc.vector.scalar_tensor_tensor(
                out=dst, in0=hb[(g, b)][:], scalar=w_f[:, 1:2], in1=prev, op0=ALU.mult, op1=ALU.add
            )

        def do_accG(g, b):
            dst, prev = acc_parts(g, b)
            h1w[(g, b)] = keep.tile([P, 4, P], F32, name="h1w%d%d" % (g, b))
            nc.scalar.activation(out=h1w[(g, b)][:], in_=hb[(g, b)][:], func=ACT.Copy, scale=w_f[:, 1:2])
            nc.gpsimd.tensor_tensor(out=dst, in0=h1w[(g, b)][:], in1=prev, op=ALU.add)

        def do_hq(g, h):
            h_codes[(g, h)] = keep.tile([P, H], U32, name="h_codes%d%d" % (g, h), align_bytes=64)
            h_scales[(g, h)] = keep.tile([P, H], U8, name="h_scales%d%d" % (g, h), align_bytes=64)
            nc.vector.quantize_mx(
                out=h_codes[(g, h)][:].bitcast(FP8X4),
                scales=h_scales[(g, h)][:],
                in_=hg[(g, h)][:].rearrange("p d t -> p (d t)"),
            )

        ob = {}
        o_sb = {}

        def do_O(h, c):
            ob[(h, c)] = psum.tile([P, 2, H], F32, tag="bank%d" % len(ob), name="ob%d%d" % (h, c))
            for e in range(2):
                for gp in range(2):
                    lt, ls = lhs(2 * c + e, gp)
                    nc.tensor.matmul_mx(
                        out=ob[(h, c)][:, e, :],
                        lhsT=lt,
                        lhsT_scale=ls,
                        rhs=h_codes[(gp, h)][:].bitcast(FP8X4),
                        rhs_scale=h_scales[(gp, h)][:],
                        start=(gp == 0),
                        stop=(gp == 1),
                    )

        def do_fin(path, h, c):
            g, u = divmod(c, 2)
            if c not in o_sb:
                o_sb[c] = keep.tile([P, 2, D], F32, name="o%d" % c)
            o = o_sb[c][:, :, H * h : H * (h + 1)]
            prev = acc[(g, h)][:, 2 * u : 2 * u + 2, :]
            if path == "V":
                nc.vector.scalar_tensor_tensor(
                    out=o, in0=ob[(h, c)][:], scalar=w_f[:, 2:3], in1=prev, op0=ALU.mult, op1=ALU.add
                )
            else:
                h2w = keep.tile([P, 2, H], F32, name="h2w%d%d" % (h, c))
                nc.scalar.activation(out=h2w[:], in_=ob[(h, c)][:], func=ACT.Copy, scale=w_f[:, 2:3])
                nc.gpsimd.tensor_tensor(out=o, in0=h2w[:], in1=prev, op=ALU.add)

        def do_st(c, lo, hi):
            g, u = divmod(c, 2)
            rows = out[512 * g : 512 * (g + 1), lo:hi].rearrange("(p t) d -> p t d", t=4)
            nc.sync.dma_start(out=rows[:, 2 * u : 2 * u + 2, :], in_=o_sb[c][:, :, lo:hi])

        do_W(7)
        do_xrg("V", 0, 0)
        do_xrg("S", 0, 1)
        nc.vector.tensor_copy(out=w_f[:], in_=w_bf[:])
        do_w0x("V", 0, 0)
        do_xq(0, 0)
        do_T(0)
        do_T(1)
        do_AT("S", 0)
        do_AT("S", 1)
        do_xq(0, 1)
        do_w0x("V", 0, 1)
        do_W(2)
        do_T(2)
        do_T(3)
        do_AT("S", 2)
        do_AT("S", 3)
        do_Aq(0)
        do_T(4)
        do_T(5)
        do_AT("S", 4)
        do_AT("S", 5)
        do_xrg("V", 1, 0)
        do_Aq(1)
        do_xq(1, 0)
        do_xrg("V", 1, 1)
        do_W(2)
        do_T(6)
        do_T(7)
        do_AT("S", 6)
        do_AT("S", 7)
        do_Aq(2)
        do_xq(1, 1)
        do_Aq(3)
        nc.vector.tensor_copy(out=w_g[:], in_=w_f[:])
        do_w0x("G", 1, 0)
        do_w0x("G", 1, 1)

        for b in range(4):
            do_M(0, b)
            do_h1c("S", 0, b)
        do_acc(0, 0)
        do_acc(0, 1)
        do_hq(0, 0)
        do_acc(0, 2)
        do_acc(0, 3)
        for b in range(4):
            do_M(1, b)
        do_h1c("S", 1, 0)
        do_h1c("S", 1, 1)
        do_accG(1, 1)
        do_hq(1, 0)
        do_hq(0, 1)
        do_acc(1, 0)
        do_h1c("S", 1, 2)
        do_h1c("S", 1, 3)
        do_O(0, 0)
        do_fin("V", 0, 0)
        do_st(0, 0, H)
        do_hq(1, 1)
        do_accG(1, 2)
        do_accG(1, 3)
        do_O(0, 1)
        do_fin("V", 0, 1)
        do_st(1, 0, H)
        do_O(0, 2)
        do_fin("V", 0, 2)
        do_st(2, 0, H)
        do_O(0, 3)
        do_fin("V", 0, 3)
        do_st(3, 0, H)
        do_O(1, 0)
        do_fin("V", 1, 0)
        do_st(0, H, D)
        do_O(1, 1)
        do_fin("V", 1, 1)
        do_st(1, H, D)
        do_O(1, 2)
        do_fin("V", 1, 2)
        do_st(2, H, D)
        do_O(1, 3)
        do_fin("V", 1, 3)
        do_st(3, H, D)
